import numpy as np
import ml_dtypes

BF16 = ml_dtypes.bfloat16


def bf(x):
    return np.asarray(x, np.float32).astype(BF16)


def f32(x):
    return np.asarray(x, np.float32)


def f64(x):
    return np.asarray(x).astype(np.float64)


def striped(idx):
    return np.tile(idx.reshape(-1, 16).T, (8, 1))


T, K, S, N = 512, 512, 512, 256
ALPHA = 0.75


def setup_inputs():
    return {"base": f32(np.random.standard_normal((T, S))), "x": bf(np.random.standard_normal((K, T))), "w": bf(np.random.standard_normal((K, N)) / np.sqrt(K)), "scale": f32(1.0 + 0.1 * np.random.standard_normal((1, N))), "bias": f32(0.1 * np.random.standard_normal((1, N))), "offs": striped(np.random.permutation(S)[:N])}


def reference(base, x, w, scale, bias, offs):
    idx = offs[:16].T.reshape(-1)
    y = f64(x).T @ f64(w)
    out = f64(base).copy()
    out[:, idx] = y * (ALPHA * f64(scale)) + f64(bias)
    return out

@@ -1,0 +1,58 @@
+import concourse.mybir as mybir
+
+P = 128
+T, K, S, N = 512, 512, 512, 256
+ALPHA = 0.75
+T_BLOCKS = T // P
+K_BLOCKS = K // P
+FLOPS = 2 * T * K * N
+
+BF16, F32, U16 = mybir.dt.bfloat16, mybir.dt.float32, mybir.dt.uint16
+MULT, ADD = mybir.AluOpType.mult, mybir.AluOpType.add
+
+
+def tile_tuckerlinear_kernel(tc, base, x, w, scale, bias, offs, out):
+    nc = tc.nc
+    with (
+        tc.tile_pool(name="held", bufs=1) as held,
+        tc.tile_pool(name="work", bufs=2) as work,
+        tc.psum_pool(name="psum", bufs=1) as psum,
+    ):
+        offsets = held.tile([P, N // 16], U16, name="offsets")
+        nc.sync.dma_start(offsets[:], offs)
+
+        x_sb = held.tile([P, K_BLOCKS, T], BF16, name="x_sb")
+        w_sb = held.tile([P, K_BLOCKS, N], BF16, name="w_sb")
+        nc.sync.dma_start(x_sb[:], x.rearrange("(kb p) t -> p kb t", p=P))
+        nc.scalar.dma_start(w_sb[:], w.rearrange("(kb p) n -> p kb n", p=P))
+
+        scale_all = held.tile([P, N], F32, name="scale_all")
+        bias_all = held.tile([P, N], F32, name="bias_all")
+        nc.scalar.dma_start(scale_all[:], scale.to_broadcast([P, N]))
+        nc.scalar.dma_start(bias_all[:], bias.to_broadcast([P, N]))
+
+        windows = [held.tile([P, S], F32, name=f"window{tb}") for tb in range(T_BLOCKS)]
+        for tb in range(T_BLOCKS):
+            queue = nc.sync if tb % 2 == 0 else nc.scalar
+            queue.dma_start(windows[tb][:], base[tb * P : (tb + 1) * P, :])
+
+        gain_all = held.tile([P, N], F32, name="gain_all")
+        nc.vector.tensor_scalar_mul(gain_all[:], scale_all[:], ALPHA)
+
+        products = [psum.tile([P, N], F32, name=f"product{tb}") for tb in range(T_BLOCKS)]
+        for tb in range(T_BLOCKS):
+            for kb in range(K_BLOCKS):
+                nc.tensor.matmul(
+                    products[tb][:],
+                    x_sb[:, kb, tb * P : (tb + 1) * P],
+                    w_sb[:, kb, :],
+                    start=(kb == 0),
+                    stop=(kb == K_BLOCKS - 1),
+                )
+
+        for tb in range(T_BLOCKS):
+            scaled = work.tile([P, N], F32, name="scaled")
+            nc.vector.tensor_tensor(scaled[:], products[tb][:], gain_all[:], MULT)
+            nc.vector.tensor_tensor(windows[tb][:].indirect(offsets[:]), scaled[:], bias_all[:], ADD)
+            queue = nc.sync if tb % 2 == 0 else nc.scalar
+            queue.dma_start(out[tb * P : (tb + 1) * P, :], windows[tb][:])

@@ -15,44 +15,45 @@ def tile_tuckerlinear_kernel(tc, base, x, w, scale, bias, offs, out):
     nc = tc.nc
     with (
         tc.tile_pool(name="held", bufs=1) as held,
-        tc.tile_pool(name="work", bufs=2) as work,
-        tc.psum_pool(name="psum", bufs=1) as psum,
+        tc.tile_pool(name="blocks", bufs=T_BLOCKS) as blocks,
+        tc.psum_pool(name="psum", bufs=T_BLOCKS) as psum,
     ):
         offsets = held.tile([P, N // 16], U16, name="offsets")
         nc.sync.dma_start(offsets[:], offs)
 
-        x_sb = held.tile([P, K_BLOCKS, T], BF16, name="x_sb")
         w_sb = held.tile([P, K_BLOCKS, N], BF16, name="w_sb")
-        nc.sync.dma_start(x_sb[:], x.rearrange("(kb p) t -> p kb t", p=P))
         nc.scalar.dma_start(w_sb[:], w.rearrange("(kb p) n -> p kb n", p=P))
 
         scale_all = held.tile([P, N], F32, name="scale_all")
         bias_all = held.tile([P, N], F32, name="bias_all")
-        nc.scalar.dma_start(scale_all[:], scale.to_broadcast([P, N]))
-        nc.scalar.dma_start(bias_all[:], bias.to_broadcast([P, N]))
 
-        windows = [held.tile([P, S], F32, name=f"window{tb}") for tb in range(T_BLOCKS)]
+        x_blocks, windows = [], []
         for tb in range(T_BLOCKS):
-            queue = nc.sync if tb % 2 == 0 else nc.scalar
-            queue.dma_start(windows[tb][:], base[tb * P : (tb + 1) * P, :])
+            tokens = slice(tb * P, (tb + 1) * P)
+            x_block = blocks.tile([P, K_BLOCKS, P], BF16, name="x_block")
+            nc.sync.dma_start(x_block[:], x[:, tokens].rearrange("(kb p) t -> p kb t", p=P))
+            if tb == 0:
+                nc.sync.dma_start(scale_all[:], scale.to_broadcast([P, N]))
+                nc.scalar.dma_start(bias_all[:], bias.to_broadcast([P, N]))
+            window = blocks.tile([P, S], F32, name="window")
+            nc.sync.dma_start(window[:], base[tokens, :])
+            x_blocks.append(x_block)
+            windows.append(window)
 
         gain_all = held.tile([P, N], F32, name="gain_all")
         nc.vector.tensor_scalar_mul(gain_all[:], scale_all[:], ALPHA)
 
-        products = [psum.tile([P, N], F32, name=f"product{tb}") for tb in range(T_BLOCKS)]
         for tb in range(T_BLOCKS):
+            product = psum.tile([P, N], F32, name="product")
             for kb in range(K_BLOCKS):
                 nc.tensor.matmul(
-                    products[tb][:],
-                    x_sb[:, kb, tb * P : (tb + 1) * P],
+                    product[:],
+                    x_blocks[tb][:, kb, :],
                     w_sb[:, kb, :],
                     start=(kb == 0),
                     stop=(kb == K_BLOCKS - 1),
                 )
-
-        for tb in range(T_BLOCKS):
-            scaled = work.tile([P, N], F32, name="scaled")
-            nc.vector.tensor_tensor(scaled[:], products[tb][:], gain_all[:], MULT)
+            scaled = blocks.tile([P, N], F32, name="scaled")
+            nc.vector.tensor_tensor(scaled[:], product[:], gain_all[:], MULT)
             nc.vector.tensor_tensor(windows[tb][:].indirect(offsets[:]), scaled[:], bias_all[:], ADD)
-            queue = nc.sync if tb % 2 == 0 else nc.scalar
-            queue.dma_start(out[tb * P : (tb + 1) * P, :], windows[tb][:])
+            nc.scalar.dma_start(out[tb * P : (tb + 1) * P, :], windows[tb][:])

@@ -27,23 +27,29 @@ def tile_tuckerlinear_kernel(tc, base, x, w, scale, bias, offs, out):
         scale_all = held.tile([P, N], F32, name="scale_all")
         bias_all = held.tile([P, N], F32, name="bias_all")
 
-        x_blocks, windows = [], []
-        for tb in range(T_BLOCKS):
+        x_blocks = [blocks.tile([P, K_BLOCKS, P], BF16, name="x_block") for tb in range(T_BLOCKS)]
+        windows = [blocks.tile([P, S], F32, name="window") for tb in range(T_BLOCKS)]
+
+        def load_x(tb):
             tokens = slice(tb * P, (tb + 1) * P)
-            x_block = blocks.tile([P, K_BLOCKS, P], BF16, name="x_block")
-            nc.sync.dma_start(x_block[:], x[:, tokens].rearrange("(kb p) t -> p kb t", p=P))
-            if tb == 0:
-                nc.sync.dma_start(scale_all[:], scale.to_broadcast([P, N]))
-                nc.scalar.dma_start(bias_all[:], bias.to_broadcast([P, N]))
-            window = blocks.tile([P, S], F32, name="window")
-            nc.sync.dma_start(window[:], base[tokens, :])
-            x_blocks.append(x_block)
-            windows.append(window)
+            nc.sync.dma_start(x_blocks[tb][:], x[:, tokens].rearrange("(kb p) t -> p kb t", p=P))
+
+        def load_window(tb):
+            nc.sync.dma_start(windows[tb][:], base[tb * P : (tb + 1) * P, :])
+
+        load_x(0)
+        nc.sync.dma_start(scale_all[:], scale.to_broadcast([P, N]))
+        nc.scalar.dma_start(bias_all[:], bias.to_broadcast([P, N]))
+        load_window(0)
+        for tb in range(1, T_BLOCKS):
+            load_x(tb)
+        for tb in range(1, T_BLOCKS):
+            load_window(tb)
 
         gain_all = held.tile([P, N], F32, name="gain_all")
         nc.vector.tensor_scalar_mul(gain_all[:], scale_all[:], ALPHA)
 
-        for tb in range(T_BLOCKS):
+        def scaled_product(tb):
             product = psum.tile([P, N], F32, name="product")
             for kb in range(K_BLOCKS):
                 nc.tensor.matmul(
@@ -55,5 +61,12 @@ def tile_tuckerlinear_kernel(tc, base, x, w, scale, bias, offs, out):
                 )
             scaled = blocks.tile([P, N], F32, name="scaled")
             nc.vector.tensor_tensor(scaled[:], product[:], gain_all[:], MULT)
+            return scaled
+
+        scaled_next = scaled_product(0)
+        for tb in range(T_BLOCKS):
+            scaled = scaled_next
+            if tb + 1 < T_BLOCKS:
+                scaled_next = scaled_product(tb + 1)
             nc.vector.tensor_tensor(windows[tb][:].indirect(offsets[:]), scaled[:], bias_all[:], ADD)
             nc.scalar.dma_start(out[tb * P : (tb + 1) * P, :], windows[tb][:])

@@ -18,14 +18,15 @@ def tile_tuckerlinear_kernel(tc, base, x, w, scale, bias, offs, out):
         tc.tile_pool(name="blocks", bufs=T_BLOCKS) as blocks,
         tc.psum_pool(name="psum", bufs=T_BLOCKS) as psum,
     ):
+        rows = held.tile([1, 2 * N], F32, name="rows")
+        nc.sync.dma_start(rows[:, 0:N], scale)
+        nc.scalar.dma_start(rows[:, N : 2 * N], bias)
+
         offsets = held.tile([P, N // 16], U16, name="offsets")
         nc.sync.dma_start(offsets[:], offs)
 
         w_sb = held.tile([P, K_BLOCKS, N], BF16, name="w_sb")
         nc.scalar.dma_start(w_sb[:], w.rearrange("(kb p) n -> p kb n", p=P))
-
-        scale_all = held.tile([P, N], F32, name="scale_all")
-        bias_all = held.tile([P, N], F32, name="bias_all")
 
         x_blocks = [blocks.tile([P, K_BLOCKS, P], BF16, name="x_block") for tb in range(T_BLOCKS)]
         windows = [blocks.tile([P, S], F32, name="window") for tb in range(T_BLOCKS)]
@@ -38,16 +39,20 @@ def tile_tuckerlinear_kernel(tc, base, x, w, scale, bias, offs, out):
             nc.sync.dma_start(windows[tb][:], base[tb * P : (tb + 1) * P, :])
 
         load_x(0)
-        nc.sync.dma_start(scale_all[:], scale.to_broadcast([P, N]))
-        nc.scalar.dma_start(bias_all[:], bias.to_broadcast([P, N]))
         load_window(0)
         for tb in range(1, T_BLOCKS):
             load_x(tb)
         for tb in range(1, T_BLOCKS):
             load_window(tb)
 
+        ones = held.tile([1, P], F32, name="ones")
+        nc.vector.memset(ones[:], 1.0)
+        rows_all = psum.tile([P, 2 * N], F32, name="rows_all", bufs=1)
+        nc.tensor.matmul(rows_all[:], ones[:], rows[:], start=True, stop=True)
         gain_all = held.tile([P, N], F32, name="gain_all")
-        nc.vector.tensor_scalar_mul(gain_all[:], scale_all[:], ALPHA)
+        bias_all = held.tile([P, N], F32, name="bias_all")
+        nc.vector.tensor_scalar_mul(gain_all[:], rows_all[:, 0:N], ALPHA)
+        nc.vector.tensor_copy(bias_all[:], rows_all[:, N : 2 * N])
 
         def scaled_product(tb):
             product = psum.tile([P, N], F32, name="product")

@@ -6,6 +6,8 @@ ALPHA = 0.75
 T_BLOCKS = T // P
 K_BLOCKS = K // P
 FLOPS = 2 * T * K * N
+BANK = 512
+WARM_MATMULS = 6
 
 BF16, F32, U16 = mybir.dt.bfloat16, mybir.dt.float32, mybir.dt.uint16
 MULT, ADD = mybir.AluOpType.mult, mybir.AluOpType.add
@@ -18,6 +20,12 @@ def tile_tuckerlinear_kernel(tc, base, x, w, scale, bias, offs, out):
         tc.tile_pool(name="blocks", bufs=T_BLOCKS) as blocks,
         tc.psum_pool(name="psum", bufs=T_BLOCKS) as psum,
     ):
+        zeros = held.tile([P, BANK], BF16, name="zeros")
+        nc.gpsimd.memset(zeros[:], 0.0)
+        unread = psum.tile([P, BANK], F32, name="unread", bufs=1)
+        for repeat in range(WARM_MATMULS):
+            nc.tensor.matmul(unread[:], zeros[:, 0:P], zeros[:], start=True, stop=True)
+
         rows = held.tile([1, 2 * N], F32, name="rows")
         nc.sync.dma_start(rows[:, 0:N], scale)
         nc.scalar.dma_start(rows[:, N : 2 * N], bias)

@@ -1,16 +1,19 @@
 import concourse.mybir as mybir
 
 P = 128
+QUAD = 32
 T, K, S, N = 512, 512, 512, 256
 ALPHA = 0.75
 T_BLOCKS = T // P
 K_BLOCKS = K // P
 FLOPS = 2 * T * K * N
-BANK = 512
-WARM_MATMULS = 6
 
 BF16, F32, U16 = mybir.dt.bfloat16, mybir.dt.float32, mybir.dt.uint16
 MULT, ADD = mybir.AluOpType.mult, mybir.AluOpType.add
+
+
+def by_blocks(tile):
+    return tile[:].rearrange("p (b k) -> p b k", k=QUAD)
 
 
 def tile_tuckerlinear_kernel(tc, base, x, w, scale, bias, offs, out):
@@ -20,15 +23,13 @@ def tile_tuckerlinear_kernel(tc, base, x, w, scale, bias, offs, out):
         tc.tile_pool(name="blocks", bufs=T_BLOCKS) as blocks,
         tc.psum_pool(name="psum", bufs=T_BLOCKS) as psum,
     ):
-        zeros = held.tile([P, BANK], BF16, name="zeros")
-        nc.gpsimd.memset(zeros[:], 0.0)
-        unread = psum.tile([P, BANK], F32, name="unread", bufs=1)
-        for repeat in range(WARM_MATMULS):
-            nc.tensor.matmul(unread[:], zeros[:, 0:P], zeros[:], start=True, stop=True)
-
-        rows = held.tile([1, 2 * N], F32, name="rows")
-        nc.sync.dma_start(rows[:, 0:N], scale)
-        nc.scalar.dma_start(rows[:, N : 2 * N], bias)
+        names = ("gain", "bias")
+        factors = (ALPHA, 1.0)
+        seeded = [held.tile([P, N], F32, name=f"{name}_seeded", align_bytes=64) for name in names]
+        for tile, row, queue in zip(seeded, (scale, bias), (nc.sync, nc.scalar)):
+            nc.vector.memset(tile[:], 0.0)
+            first_partitions = tile[:].rearrange("(q i) n -> q i n", i=QUAD)[:, 0, :]
+            queue.dma_start(first_partitions, row.to_broadcast([P // QUAD, N]))
 
         offsets = held.tile([P, N // 16], U16, name="offsets")
         nc.sync.dma_start(offsets[:], offs)
@@ -53,14 +54,17 @@ def tile_tuckerlinear_kernel(tc, base, x, w, scale, bias, offs, out):
         for tb in range(1, T_BLOCKS):
             load_window(tb)
 
-        ones = held.tile([1, P], F32, name="ones")
-        nc.vector.memset(ones[:], 1.0)
-        rows_all = psum.tile([P, 2 * N], F32, name="rows_all", bufs=1)
-        nc.tensor.matmul(rows_all[:], ones[:], rows[:], start=True, stop=True)
-        gain_all = held.tile([P, N], F32, name="gain_all")
-        bias_all = held.tile([P, N], F32, name="bias_all")
-        nc.vector.tensor_scalar_mul(gain_all[:], rows_all[:, 0:N], ALPHA)
-        nc.vector.tensor_copy(bias_all[:], rows_all[:, N : 2 * N])
+        turned = [held.tile([P, N], F32, name=f"{name}_turned", align_bytes=64) for name in names]
+        for r in range(len(names)):
+            nc.vector.transpose(turned[r][:], seeded[r][:])
+        widened = [held.tile([P, N], F32, name=f"{name}_widened", align_bytes=64) for name in names]
+        for r in range(len(names)):
+            column0 = by_blocks(turned[r])[:, :, 0:1].to_broadcast([P, N // QUAD, QUAD])
+            nc.vector.tensor_scalar_mul(by_blocks(widened[r]), column0, factors[r])
+        spread = [held.tile([P, N], F32, name=f"{name}_all", align_bytes=64) for name in names]
+        for r in range(len(names)):
+            nc.vector.transpose(spread[r][:], widened[r][:])
+        gain_all, bias_all = spread
 
         def scaled_product(tb):
             product = psum.tile([P, N], F32, name="product")

@@ -27,15 +27,13 @@ def tile_tuckerlinear_kernel(tc, base, x, w, scale, bias, offs, out):
         factors = (ALPHA, 1.0)
         seeded = [held.tile([P, N], F32, name=f"{name}_seeded", align_bytes=64) for name in names]
         for tile, row, queue in zip(seeded, (scale, bias), (nc.sync, nc.scalar)):
-            nc.vector.memset(tile[:], 0.0)
+            nc.gpsimd.memset(tile[:], 0.0)
             first_partitions = tile[:].rearrange("(q i) n -> q i n", i=QUAD)[:, 0, :]
             queue.dma_start(first_partitions, row.to_broadcast([P // QUAD, N]))
 
         offsets = held.tile([P, N // 16], U16, name="offsets")
-        nc.sync.dma_start(offsets[:], offs)
-
         w_sb = held.tile([P, K_BLOCKS, N], BF16, name="w_sb")
-        nc.scalar.dma_start(w_sb[:], w.rearrange("(kb p) n -> p kb n", p=P))
+        w_by_blocks = w.rearrange("(kb p) n -> p kb n", p=P)
 
         x_blocks = [blocks.tile([P, K_BLOCKS, P], BF16, name="x_block") for tb in range(T_BLOCKS)]
         windows = [blocks.tile([P, S], F32, name="window") for tb in range(T_BLOCKS)]
@@ -48,6 +46,9 @@ def tile_tuckerlinear_kernel(tc, base, x, w, scale, bias, offs, out):
             nc.sync.dma_start(windows[tb][:], base[tb * P : (tb + 1) * P, :])
 
         load_x(0)
+        for half in (slice(0, K_BLOCKS // 2), slice(K_BLOCKS // 2, K_BLOCKS)):
+            nc.sync.dma_start(w_sb[:, half, :], w_by_blocks[:, half, :])
+        nc.sync.dma_start(offsets[:], offs)
         load_window(0)
         for tb in range(1, T_BLOCKS):
             load_x(tb)

@@ -26,10 +26,8 @@ def tile_tuckerlinear_kernel(tc, base, x, w, scale, bias, offs, out):
         names = ("gain", "bias")
         factors = (ALPHA, 1.0)
         seeded = [held.tile([P, N], F32, name=f"{name}_seeded", align_bytes=64) for name in names]
-        for tile, row, queue in zip(seeded, (scale, bias), (nc.sync, nc.scalar)):
-            nc.gpsimd.memset(tile[:], 0.0)
-            first_partitions = tile[:].rearrange("(q i) n -> q i n", i=QUAD)[:, 0, :]
-            queue.dma_start(first_partitions, row.to_broadcast([P // QUAD, N]))
+        for tile, engine in zip(seeded, (nc.vector, nc.gpsimd)):
+            engine.memset(tile[:], 0.0)
 
         offsets = held.tile([P, N // 16], U16, name="offsets")
         w_sb = held.tile([P, K_BLOCKS, N], BF16, name="w_sb")
@@ -45,7 +43,13 @@ def tile_tuckerlinear_kernel(tc, base, x, w, scale, bias, offs, out):
         def load_window(tb):
             nc.sync.dma_start(windows[tb][:], base[tb * P : (tb + 1) * P, :])
 
+        def load_row(tile, row, queue):
+            first_partitions = tile[:].rearrange("(q i) n -> q i n", i=QUAD)[:, 0, :]
+            queue.dma_start(first_partitions, row.to_broadcast([P // QUAD, N]))
+
         load_x(0)
+        load_row(seeded[0], scale, nc.scalar)
+        load_row(seeded[1], bias, nc.sync)
         for half in (slice(0, K_BLOCKS // 2), slice(K_BLOCKS // 2, K_BLOCKS)):
             nc.sync.dma_start(w_sb[:, half, :], w_by_blocks[:, half, :])
         nc.sync.dma_start(offsets[:], offs)

@@ -31,14 +31,14 @@ def tile_tuckerlinear_kernel(tc, base, x, w, scale, bias, offs, out):
 
         offsets = held.tile([P, N // 16], U16, name="offsets")
         w_sb = held.tile([P, K_BLOCKS, N], BF16, name="w_sb")
-        w_by_blocks = w.rearrange("(kb p) n -> p kb n", p=P)
+        w_by_blocks = w.rearrange("(p kb) n -> p kb n", kb=K_BLOCKS)
 
         x_blocks = [blocks.tile([P, K_BLOCKS, P], BF16, name="x_block") for tb in range(T_BLOCKS)]
         windows = [blocks.tile([P, S], F32, name="window") for tb in range(T_BLOCKS)]
 
         def load_x(tb):
             tokens = slice(tb * P, (tb + 1) * P)
-            nc.sync.dma_start(x_blocks[tb][:], x[:, tokens].rearrange("(kb p) t -> p kb t", p=P))
+            nc.sync.dma_start(x_blocks[tb][:], x[:, tokens].rearrange("(p kb) t -> p kb t", kb=K_BLOCKS))
 
         def load_window(tb):
             nc.sync.dma_start(windows[tb][:], base[tb * P : (tb + 1) * P, :])

import concourse.mybir as mybir

P = 128
QUAD = 32
T, K, S, N = 512, 512, 512, 256
ALPHA = 0.75
T_BLOCKS = T // P
K_BLOCKS = K // P
FLOPS = 2 * T * K * N

BF16, F32, U16 = mybir.dt.bfloat16, mybir.dt.float32, mybir.dt.uint16
MULT, ADD = mybir.AluOpType.mult, mybir.AluOpType.add


def by_blocks(tile):
    return tile[:].rearrange("p (b k) -> p b k", k=QUAD)


def tile_tuckerlinear_kernel(tc, base, x, w, scale, bias, offs, out):
    nc = tc.nc
    with (
        tc.tile_pool(name="held", bufs=1) as held,
        tc.tile_pool(name="blocks", bufs=T_BLOCKS) as blocks,
        tc.psum_pool(name="psum", bufs=T_BLOCKS) as psum,
    ):
        names = ("gain", "bias")
        factors = (ALPHA, 1.0)
        seeded = [held.tile([P, N], F32, name=f"{name}_seeded", align_bytes=64) for name in names]
        for tile, engine in zip(seeded, (nc.vector, nc.gpsimd)):
            engine.memset(tile[:], 0.0)

        offsets = held.tile([P, N // 16], U16, name="offsets")
        w_sb = held.tile([P, K_BLOCKS, N], BF16, name="w_sb")
        w_by_blocks = w.rearrange("(p kb) n -> p kb n", kb=K_BLOCKS)

        x_blocks = [blocks.tile([P, K_BLOCKS, P], BF16, name="x_block") for tb in range(T_BLOCKS)]
        windows = [blocks.tile([P, S], F32, name="window") for tb in range(T_BLOCKS)]

        def load_x(tb):
            tokens = slice(tb * P, (tb + 1) * P)
            nc.sync.dma_start(x_blocks[tb][:], x[:, tokens].rearrange("(p kb) t -> p kb t", kb=K_BLOCKS))

        def load_window(tb):
            nc.sync.dma_start(windows[tb][:], base[tb * P : (tb + 1) * P, :])

        def load_row(tile, row, queue):
            first_partitions = tile[:].rearrange("(q i) n -> q i n", i=QUAD)[:, 0, :]
            queue.dma_start(first_partitions, row.to_broadcast([P // QUAD, N]))

        load_x(0)
        load_row(seeded[0], scale, nc.scalar)
        load_row(seeded[1], bias, nc.sync)
        for half in (slice(0, K_BLOCKS // 2), slice(K_BLOCKS // 2, K_BLOCKS)):
            nc.sync.dma_start(w_sb[:, half, :], w_by_blocks[:, half, :])
        nc.sync.dma_start(offsets[:], offs)
        load_window(0)
        for tb in range(1, T_BLOCKS):
            load_x(tb)
        for tb in range(1, T_BLOCKS):
            load_window(tb)

        turned = [held.tile([P, N], F32, name=f"{name}_turned", align_bytes=64) for name in names]
        for r in range(len(names)):
            nc.vector.transpose(turned[r][:], seeded[r][:])
        widened = [held.tile([P, N], F32, name=f"{name}_widened", align_bytes=64) for name in names]
        for r in range(len(names)):
            column0 = by_blocks(turned[r])[:, :, 0:1].to_broadcast([P, N // QUAD, QUAD])
            nc.vector.tensor_scalar_mul(by_blocks(widened[r]), column0, factors[r])
        spread = [held.tile([P, N], F32, name=f"{name}_all", align_bytes=64) for name in names]
        for r in range(len(names)):
            nc.vector.transpose(spread[r][:], widened[r][:])
        gain_all, bias_all = spread

        def scaled_product(tb):
            product = psum.tile([P, N], F32, name="product")
            for kb in range(K_BLOCKS):
                nc.tensor.matmul(
                    product[:],
                    x_blocks[tb][:, kb, :],
                    w_sb[:, kb, :],
                    start=(kb == 0),
                    stop=(kb == K_BLOCKS - 1),
                )
            scaled = blocks.tile([P, N], F32, name="scaled")
            nc.vector.tensor_tensor(scaled[:], product[:], gain_all[:], MULT)
            return scaled

        scaled_next = scaled_product(0)
        for tb in range(T_BLOCKS):
            scaled = scaled_next
            if tb + 1 < T_BLOCKS:
                scaled_next = scaled_product(tb + 1)
            nc.vector.tensor_tensor(windows[tb][:].indirect(offsets[:]), scaled[:], bias_all[:], ADD)
            nc.scalar.dma_start(out[tb * P : (tb + 1) * P, :], windows[tb][:])
